import numpy as np
import ml_dtypes


def mxq(x, axis, fmt="e4m3"):
    dtype, down = {"e4m3": (ml_dtypes.float8_e4m3fn, 7), "e5m2": (ml_dtypes.float8_e5m2, 14)}[fmt]
    v = np.moveaxis(np.asarray(x, np.float32).astype(ml_dtypes.bfloat16).astype(np.float64), axis, -1)
    blocks = v.reshape(v.shape[:-1] + (-1, 32))
    amax = np.abs(blocks).max(-1, keepdims=True)
    byte = np.maximum(np.where(amax > 0, np.frexp(amax)[1] - 1 + 127, 0) - down, 1)
    scale = np.exp2(byte - 127.0)
    codes = (blocks / scale).astype(np.float32).astype(dtype).astype(np.float64)
    return np.moveaxis((codes * scale).reshape(v.shape), -1, axis)


WIDE = False


def mx_kscale(k):
    if not WIDE:
        return np.ones(k)
    levels = np.array([10, -10, 5, -5, 0])
    if k % 512:
        return np.exp2(np.random.permutation(np.resize(levels, k // 32))).repeat(32)
    a = np.empty((k // 512, 16))
    for p in range(k // 512):
        a[p, :8] = np.random.permutation(np.resize(levels, 8))
        for g in range(8):
            far = levels[np.abs(levels - a[p, g]) >= 10]
            a[p, g + 8] = far[np.random.randint(len(far))]
    return np.exp2(a.ravel()).repeat(32)


BF16 = ml_dtypes.bfloat16


def bf(x):
    return np.asarray(x, np.float32).astype(BF16)


def f64(x):
    return np.asarray(x).astype(np.float64)


B, T, D, H, DH, F = 4, 1024, 512, 16, 64, 256
A = H * DH
EPS = 1e-6


def layer_norm(v, gain, bias):
    mu = v.mean(-1, keepdims=True)
    var = np.square(v - mu).mean(-1, keepdims=True)
    return (v - mu) * (1.0 / np.sqrt(var + EPS)) * gain + bias


def gelu_tanh(v):
    return 0.5 * v * (1.0 + np.tanh(np.sqrt(2.0 / np.pi) * (v + 0.044715 * v**3)))


def setup_inputs():
    s, t = mx_kscale(A), mx_kscale(D)
    r = np.random.standard_normal
    return {"attn_out": bf(r((B, T, A)) * 0.3 * s),
            "residual": bf(r((B, T, D))),
            "wo": bf(r((A, D)) * 2.0 / np.sqrt(A) / s[:, None]),
            "bo": bf(0.1 * r(D)),
            "ln2_gain": bf((1.0 + 0.1 * r(D)) * t),
            "ln2_bias": bf(0.1 * r(D) * t),
            "w1": bf(r((D, F)) / np.sqrt(D) / t[:, None]),
            "b1": bf(0.1 * r(F))}


def reference(attn_out, residual, wo, bo, ln2_gain, ln2_bias, w1, b1):
    x_mid = (mxq(f64(attn_out), 2, "e4m3") @ mxq(f64(wo), 0, "e4m3")) + f64(bo) + f64(residual)
    h = layer_norm(x_mid, f64(ln2_gain), f64(ln2_bias))
    g = gelu_tanh((mxq(h, 2, "e4m3") @ mxq(f64(w1), 0, "e4m3")) + f64(b1))
    return x_mid, g

@@ -1,0 +1,345 @@
+from contextlib import ExitStack
+
+import concourse.mybir as mybir
+from concourse.masks import make_identity
+
+F32 = mybir.dt.float32
+BF16 = mybir.dt.bfloat16
+U32 = mybir.dt.uint32
+U8 = mybir.dt.uint8
+FP8X4 = mybir.dt.float8_e4m3fn_x4
+ALU = mybir.AluOpType
+ACT = mybir.ActivationFunctionType
+
+P = 128
+PACK = 4
+K_PASS = P * PACK
+TOKENS = 4 * 1024
+A = 1024
+D = 512
+F = 256
+EPS = 1e-6
+PASSES = A // K_PASS
+UNIT_TILES = 2
+UNIT_TOKENS = UNIT_TILES * P
+UNITS = TOKENS // UNIT_TOKENS
+INPUT_BUFS = 6
+RUN = 4
+
+FLOPS = 2 * TOKENS * A * D + 2 * TOKENS * D * F
+
+
+def tile_swidtblock_pb_t_kernel(
+    tc, attn_out, residual, wo, bo, ln2_gain, ln2_bias, w1, b1, out_0, out_1
+):
+    nc = tc.nc
+    attn_units = attn_out.flatten_outer_dims().rearrange("(n p i) k -> n p (i k)", p=P, i=UNIT_TILES)
+    res_units = residual.flatten_outer_dims().rearrange("(n p i) d -> n p i d", p=P, i=UNIT_TILES)
+    x_units = out_0.flatten_outer_dims().rearrange("(n p i) d -> n p i d", p=P, i=UNIT_TILES)
+    g_units = out_1.flatten_outer_dims().rearrange("(n p i) f -> n p i f", p=P, i=UNIT_TILES)
+
+    with ExitStack() as ctx:
+        const = ctx.enter_context(tc.tile_pool(name="const", bufs=1))
+        inputs = ctx.enter_context(tc.tile_pool(name="inputs", bufs=INPUT_BUFS))
+        work = ctx.enter_context(tc.tile_pool(name="work", bufs=2))
+        held = ctx.enter_context(tc.tile_pool(name="held", bufs=3))
+        psum = ctx.enter_context(tc.psum_pool(name="psum", bufs=2))
+
+        live = {}
+
+        def load(u):
+            attn_sb = inputs.tile([P, UNIT_TILES * A], BF16)
+            nc.sync.dma_start(out=attn_sb[:], in_=attn_units[u])
+            res_sb = inputs.tile([P, UNIT_TILES, D], BF16)
+            nc.sync.dma_start(out=res_sb[:], in_=res_units[u])
+            live["attn_words", u] = attn_sb[:].bitcast(F32)
+            live["res", u] = res_sb
+
+        bias_rows = const.tile([P, D + F], BF16)
+        nc.vector.memset(bias_rows[:], 0.0)
+        nc.scalar.dma_start(out=bias_rows[0:1, 0:D], in_=bo.rearrange("(o d) -> o d", o=1))
+        nc.scalar.dma_start(out=bias_rows[0:1, D : D + F], in_=b1.rearrange("(o f) -> o f", o=1))
+        norm_raw = const.tile([P, 2, 16], BF16)
+        nc.scalar.dma_start(out=norm_raw[:, 0, 0:PACK], in_=ln2_gain.rearrange("(p t) -> p t", t=PACK))
+        nc.scalar.dma_start(out=norm_raw[:, 1, 0:PACK], in_=ln2_bias.rearrange("(p t) -> p t", t=PACK))
+        w1_raw = const.tile([P, PACK, F], BF16)
+        nc.scalar.dma_start(out=w1_raw[:], in_=w1.rearrange("(p t) f -> p t f", t=PACK))
+
+        wo_raw = const.tile([P, PASSES, PACK, D], BF16)
+        wo_rows = wo.rearrange("(s p t) c -> s p t c", s=PASSES, t=PACK)
+        for s in range(PASSES):
+            nc.sync.dma_start(out=wo_raw[:, s], in_=wo_rows[s])
+        for u in range(INPUT_BUFS):
+            load(u)
+
+        ident_f32 = const.tile([P, P], F32)
+        make_identity(nc, ident_f32[:])
+        ones = const.tile([P, P], BF16)
+        nc.vector.memset(ones[:], 1.0)
+        minus_half = const.tile([P, UNIT_TILES], F32)
+        nc.vector.memset(minus_half[:], -0.5)
+        eps_col = const.tile([P, 1], F32)
+        nc.vector.memset(eps_col[:], EPS)
+
+        def regroup(copy, grouped, planes):
+            copy(
+                out=grouped.rearrange("p (c i t) -> p c t i", i=RUN, t=PACK),
+                in_=planes.rearrange("p t (c i) -> p c t i", i=RUN),
+            )
+
+        wo_grouped = const.tile([P, PASSES, D * PACK], BF16, align_bytes=64)
+        wo_codes = const.tile([P, PASSES, D], U32, align_bytes=64)
+        wo_scales = const.tile([P, PASSES, D], U8, align_bytes=64)
+        for s in range(PASSES):
+            regroup(nc.vector.tensor_copy, wo_grouped[:, s, :], wo_raw[:, s])
+        for s in range(PASSES):
+            nc.vector.quantize_mx(
+                out=wo_codes[:, s, :].bitcast(FP8X4), scales=wo_scales[:, s, :], in_=wo_grouped[:, s, :]
+            )
+        w1_grouped = const.tile([P, F * PACK], BF16, align_bytes=64)
+        w1_codes = const.tile([P, F], U32, align_bytes=64)
+        w1_scales = const.tile([P, F], U8, align_bytes=64)
+        regroup(nc.scalar.copy, w1_grouped[:], w1_raw[:])
+        nc.vector.quantize_mx(out=w1_codes[:].bitcast(FP8X4), scales=w1_scales[:], in_=w1_grouped[:])
+
+        bo_ps = psum.tile([P, D], F32, tag="acc")
+        nc.tensor.matmul(out=bo_ps[:], lhsT=ones[:], rhs=bias_rows[:, 0:D], start=True, stop=True)
+        bo_all = const.tile([P, D], F32)
+        nc.scalar.copy(out=bo_all[:], in_=bo_ps[:])
+        b1_ps = psum.tile([P, F], F32, tag="acc")
+        nc.tensor.matmul(out=b1_ps[:], lhsT=ones[:], rhs=bias_rows[:, D : D + F], start=True, stop=True)
+        b1_all = const.tile([P, F], F32)
+        nc.scalar.copy(out=b1_all[:], in_=b1_ps[:])
+        norm_cols = const.tile([P, 2 * PACK], F32)
+        nc.scalar.copy(out=norm_cols[:].rearrange("p (g t) -> p g t", g=2), in_=norm_raw[:, :, 0:PACK])
+
+        def transpose_attn(u):
+            for i in range(UNIT_TILES):
+                at = psum.tile([P, PASSES * 2, P], F32, tag="at")
+                for s in range(PASSES):
+                    start = i * (A // 2) + s * (K_PASS // 2)
+                    for w in range(2):
+                        nc.tensor.transpose(
+                            at[:, 2 * s + w, :],
+                            live["attn_words", u][:, start + w : start + K_PASS // 2 : 2],
+                            ident_f32[:],
+                        )
+                live["at", u, i] = at
+
+        def group_attn(u):
+            a_grouped = work.tile([P, UNIT_TILES * PASSES * P * PACK], BF16, align_bytes=64)
+            words = a_grouped[:].bitcast(F32).rearrange(
+                "p (i s j u) -> p i s j u", i=UNIT_TILES, s=PASSES, u=2
+            )
+            for i in range(UNIT_TILES):
+                nc.scalar.copy(
+                    out=words[:, i], in_=live["at", u, i][:].rearrange("p (s u) j -> p s j u", u=2)
+                )
+            live["a_grouped", u] = a_grouped
+
+        def quantise_attn(u):
+            a_codes = work.tile([P, UNIT_TILES, PASSES, P], U32, align_bytes=64)
+            a_scales = work.tile([P, UNIT_TILES, PASSES, P], U8, align_bytes=64)
+            nc.vector.quantize_mx(
+                out=a_codes[:].rearrange("p i s j -> p (i s j)").bitcast(FP8X4),
+                scales=a_scales[:].rearrange("p i s j -> p (i s j)"),
+                in_=live["a_grouped", u][:],
+            )
+            live["a_codes", u] = a_codes
+            live["a_scales", u] = a_scales
+
+        def project(u):
+            for i in range(UNIT_TILES):
+                acc = psum.tile([P, D], F32, tag="acc")
+                for s in range(PASSES):
+                    nc.tensor.matmul_mx(
+                        out=acc[:],
+                        lhsT=live["a_codes", u][:, i, s, :].bitcast(FP8X4),
+                        lhsT_scale=live["a_scales", u][:, i, s, :],
+                        rhs=wo_codes[:, s, :].bitcast(FP8X4),
+                        rhs_scale=wo_scales[:, s, :],
+                        start=(s == 0),
+                        stop=(s == PASSES - 1),
+                    )
+                live["acc", u, i] = acc
+
+        def add_bias_to_residual(u):
+            res_bo = held.tile([P, UNIT_TILES, D], F32)
+            nc.vector.tensor_tensor(
+                out=res_bo[:],
+                in0=live["res", u][:],
+                in1=bo_all[:].unsqueeze(1).to_broadcast([P, UNIT_TILES, D]),
+                op=ALU.add,
+            )
+            live["res_bo", u] = res_bo
+
+        def finish_x_mid(u):
+            x_mid = held.tile([P, UNIT_TILES, D], F32)
+            row_sum = held.tile([P, UNIT_TILES], F32)
+            for i in range(UNIT_TILES):
+                nc.vector.scalar_tensor_tensor(
+                    out=x_mid[:, i, :],
+                    in0=live["acc", u, i][:],
+                    scalar=0.0,
+                    in1=live["res_bo", u][:, i, :],
+                    op0=ALU.add,
+                    op1=ALU.add,
+                    accum_out=row_sum[:, i : i + 1],
+                )
+            nc.sync.dma_start(out=x_units[u], in_=x_mid[:])
+            live["x_mid", u] = x_mid
+            live["row_sum", u] = row_sum
+
+        def negate_mean(u):
+            neg_mean = held.tile([P, UNIT_TILES], F32)
+            nc.scalar.mul(out=neg_mean[:], in_=live["row_sum", u][:], mul=-1.0 / D)
+            live["neg_mean", u] = neg_mean
+
+        def sum_squares(u):
+            sq_sum = held.tile([P, UNIT_TILES], F32)
+            for i in range(UNIT_TILES):
+                squares = work.tile([P, D], BF16)
+                nc.scalar.activation(
+                    out=squares[:],
+                    in_=live["x_mid", u][:, i, :],
+                    func=ACT.Square,
+                    bias=live["neg_mean", u][:, i : i + 1],
+                    scale=1.0,
+                    accum_out=sq_sum[:, i : i + 1],
+                )
+            live["sq_sum", u] = sq_sum
+
+        def inverse_std(u):
+            var_eps = held.tile([P, UNIT_TILES], F32)
+            nc.scalar.activation(
+                out=var_eps[:], in_=live["sq_sum", u][:], func=ACT.Identity, scale=1.0 / D, bias=eps_col[:]
+            )
+            rstd = held.tile([P, UNIT_TILES], F32)
+            nc.gpsimd.tensor_tensor(out=rstd[:], in0=var_eps[:], in1=minus_half[:], op=ALU.pow)
+            live["rstd", u] = rstd
+
+        def by_plane(rows):
+            return rows.rearrange("p (c i t) -> p c t i", i=RUN, t=PACK)
+
+        def planes_of(rows):
+            return rows.rearrange("p (t c i) -> p c t i", i=RUN, t=PACK)
+
+        def normalise_tile_0(u):
+            normed = work.tile([P, UNIT_TILES, D], F32)
+            nc.vector.tensor_scalar(
+                out=planes_of(normed[:, 0, :]),
+                in0=by_plane(live["x_mid", u][:, 0, :]),
+                scalar1=live["neg_mean", u][:, 0:1],
+                scalar2=live["rstd", u][:, 0:1],
+                op0=ALU.add,
+                op1=ALU.mult,
+            )
+            live["normed", u] = normed
+
+        def shift_of_tile_1(u):
+            shift = held.tile([P, 1], F32)
+            nc.scalar.activation(
+                out=shift[:], in_=live["neg_mean", u][:, 1:2], func=ACT.Identity, scale=live["rstd", u][:, 1:2]
+            )
+            live["shift", u] = shift
+
+        def normalise_tile_1(u):
+            nc.scalar.activation(
+                out=planes_of(live["normed", u][:, 1, :]),
+                in_=by_plane(live["x_mid", u][:, 1, :]),
+                func=ACT.Identity,
+                scale=live["rstd", u][:, 1:2],
+                bias=live["shift", u][:],
+            )
+
+        def transpose_normed(u):
+            for half in range(2):
+                planes = psum.tile([P, PACK // 2, UNIT_TILES, P], F32, tag="planes")
+                for t2 in range(PACK // 2):
+                    t = half * (PACK // 2) + t2
+                    for i in range(UNIT_TILES):
+                        nc.tensor.transpose(
+                            planes[:, t2, i, :], live["normed", u][:, i, t * P : (t + 1) * P], ident_f32[:]
+                        )
+                live["planes", u, half] = planes
+
+        def gain_and_bias(u):
+            h_planes = work.tile([P, PACK, UNIT_TOKENS], BF16)
+            for t in range(PACK):
+                nc.scalar.activation(
+                    out=h_planes[:, t, :],
+                    in_=live["planes", u, t // (PACK // 2)][:, t % (PACK // 2)].rearrange("p i j -> p (i j)"),
+                    func=ACT.Identity,
+                    scale=norm_cols[:, t : t + 1],
+                    bias=norm_cols[:, PACK + t : PACK + t + 1],
+                )
+            live["h_planes", u] = h_planes
+
+        def group_h(u):
+            h_grouped = work.tile([P, UNIT_TOKENS * PACK], BF16, align_bytes=64)
+            regroup(nc.vector.tensor_copy, h_grouped[:], live["h_planes", u][:])
+            live["h_grouped", u] = h_grouped
+
+        def quantise_h(u):
+            h_codes = work.tile([P, UNIT_TOKENS], U32, align_bytes=64)
+            h_scales = work.tile([P, UNIT_TOKENS], U8, align_bytes=64)
+            nc.vector.quantize_mx(out=h_codes[:].bitcast(FP8X4), scales=h_scales[:], in_=live["h_grouped", u][:])
+            live["h_codes", u] = h_codes
+            live["h_scales", u] = h_scales
+
+        def expand(u):
+            acc2 = psum.tile([P, UNIT_TILES, F], F32, tag="acc2")
+            for i in range(UNIT_TILES):
+                nc.tensor.matmul_mx(
+                    out=acc2[:, i, :],
+                    lhsT=live["h_codes", u][:, i * P : (i + 1) * P].bitcast(FP8X4),
+                    lhsT_scale=live["h_scales", u][:, i * P : (i + 1) * P],
+                    rhs=w1_codes[:].bitcast(FP8X4),
+                    rhs_scale=w1_scales[:],
+                    start=True,
+                    stop=True,
+                )
+            live["acc2", u] = acc2
+
+        def add_b1(u):
+            pre_gelu = work.tile([P, UNIT_TILES, F], F32)
+            nc.vector.tensor_tensor(
+                out=pre_gelu[:],
+                in0=live["acc2", u][:],
+                in1=b1_all[:].unsqueeze(1).to_broadcast([P, UNIT_TILES, F]),
+                op=ALU.add,
+            )
+            live["pre_gelu", u] = pre_gelu
+
+        def gelu_and_store(u):
+            g_sb = held.tile([P, UNIT_TILES, F], F32)
+            nc.scalar.activation(out=g_sb[:], in_=live["pre_gelu", u][:], func=ACT.Gelu_apprx_tanh)
+            nc.sync.dma_start(out=g_units[u], in_=g_sb[:])
+
+        def when_valid(stage, u):
+            if 0 <= u < UNITS:
+                stage(u)
+
+        with tc.manual_schedule():
+            for slot in range(-2, UNITS + 7):
+                if slot >= 0:
+                    when_valid(load, slot + INPUT_BUFS)
+                when_valid(project, slot)
+                when_valid(expand, slot - 5)
+                when_valid(transpose_normed, slot - 3)
+                when_valid(transpose_attn, slot + 2)
+                when_valid(normalise_tile_0, slot - 2)
+                when_valid(group_h, slot - 4)
+                when_valid(add_bias_to_residual, slot + 1)
+                when_valid(quantise_h, slot - 4)
+                when_valid(quantise_attn, slot + 1)
+                when_valid(finish_x_mid, slot)
+                when_valid(add_b1, slot - 5)
+                when_valid(negate_mean, slot - 1)
+                when_valid(shift_of_tile_1, slot - 2)
+                when_valid(gelu_and_store, slot - 6)
+                when_valid(sum_squares, slot - 1)
+                when_valid(normalise_tile_1, slot - 2)
+                when_valid(inverse_std, slot - 1)
+                when_valid(gain_and_bias, slot - 3)
+                when_valid(group_attn, slot + 2)

@@ -55,15 +55,19 @@ def tile_swidtblock_pb_t_kernel(
             live["attn_words", u] = attn_sb[:].bitcast(F32)
             live["res", u] = res_sb
 
+        gelu_probe = const.tile([P, 1], F32)
+        nc.vector.memset(gelu_probe[:], 0.0)
         bias_rows = const.tile([P, D + F], BF16)
         nc.vector.memset(bias_rows[:], 0.0)
-        nc.scalar.dma_start(out=bias_rows[0:1, 0:D], in_=bo.rearrange("(o d) -> o d", o=1))
-        nc.scalar.dma_start(out=bias_rows[0:1, D : D + F], in_=b1.rearrange("(o f) -> o f", o=1))
         norm_raw = const.tile([P, 2, 16], BF16)
         nc.scalar.dma_start(out=norm_raw[:, 0, 0:PACK], in_=ln2_gain.rearrange("(p t) -> p t", t=PACK))
         nc.scalar.dma_start(out=norm_raw[:, 1, 0:PACK], in_=ln2_bias.rearrange("(p t) -> p t", t=PACK))
         w1_raw = const.tile([P, PACK, F], BF16)
         nc.scalar.dma_start(out=w1_raw[:], in_=w1.rearrange("(p t) f -> p t f", t=PACK))
+        nc.scalar.dma_start(out=bias_rows[0:1, 0:D], in_=bo.rearrange("(o d) -> o d", o=1))
+        nc.scalar.dma_start(out=bias_rows[0:1, D : D + F], in_=b1.rearrange("(o f) -> o f", o=1))
+        gelu_done = const.tile([P, 1], F32)
+        nc.scalar.activation(out=gelu_done[:], in_=gelu_probe[:], func=ACT.Gelu_apprx_tanh)
 
         wo_raw = const.tile([P, PASSES, PACK, D], BF16)
         wo_rows = wo.rearrange("(s p t) c -> s p t c", s=PASSES, t=PACK)
@@ -113,18 +117,17 @@ def tile_swidtblock_pb_t_kernel(
         norm_cols = const.tile([P, 2 * PACK], F32)
         nc.scalar.copy(out=norm_cols[:].rearrange("p (g t) -> p g t", g=2), in_=norm_raw[:, :, 0:PACK])
 
-        def transpose_attn(u):
-            for i in range(UNIT_TILES):
-                at = psum.tile([P, PASSES * 2, P], F32, tag="at")
-                for s in range(PASSES):
-                    start = i * (A // 2) + s * (K_PASS // 2)
-                    for w in range(2):
-                        nc.tensor.transpose(
-                            at[:, 2 * s + w, :],
-                            live["attn_words", u][:, start + w : start + K_PASS // 2 : 2],
-                            ident_f32[:],
-                        )
-                live["at", u, i] = at
+        def transpose_attn(u, i):
+            at = psum.tile([P, PASSES * 2, P], F32, tag="at")
+            for s in range(PASSES):
+                start = i * (A // 2) + s * (K_PASS // 2)
+                for w in range(2):
+                    nc.tensor.transpose(
+                        at[:, 2 * s + w, :],
+                        live["attn_words", u][:, start + w : start + K_PASS // 2 : 2],
+                        ident_f32[:],
+                    )
+            live["at", u, i] = at
 
         def group_attn(u):
             a_grouped = work.tile([P, UNIT_TILES * PASSES * P * PACK], BF16, align_bytes=64)
@@ -148,20 +151,19 @@ def tile_swidtblock_pb_t_kernel(
             live["a_codes", u] = a_codes
             live["a_scales", u] = a_scales
 
-        def project(u):
-            for i in range(UNIT_TILES):
-                acc = psum.tile([P, D], F32, tag="acc")
-                for s in range(PASSES):
-                    nc.tensor.matmul_mx(
-                        out=acc[:],
-                        lhsT=live["a_codes", u][:, i, s, :].bitcast(FP8X4),
-                        lhsT_scale=live["a_scales", u][:, i, s, :],
-                        rhs=wo_codes[:, s, :].bitcast(FP8X4),
-                        rhs_scale=wo_scales[:, s, :],
-                        start=(s == 0),
-                        stop=(s == PASSES - 1),
-                    )
-                live["acc", u, i] = acc
+        def project(u, i):
+            acc = psum.tile([P, D], F32, tag="acc")
+            for s in range(PASSES):
+                nc.tensor.matmul_mx(
+                    out=acc[:],
+                    lhsT=live["a_codes", u][:, i, s, :].bitcast(FP8X4),
+                    lhsT_scale=live["a_scales", u][:, i, s, :],
+                    rhs=wo_codes[:, s, :].bitcast(FP8X4),
+                    rhs_scale=wo_scales[:, s, :],
+                    start=(s == 0),
+                    stop=(s == PASSES - 1),
+                )
+            live["acc", u, i] = acc
 
         def add_bias_to_residual(u):
             res_bo = held.tile([P, UNIT_TILES, D], F32)
@@ -252,16 +254,15 @@ def tile_swidtblock_pb_t_kernel(
                 bias=live["shift", u][:],
             )
 
-        def transpose_normed(u):
-            for half in range(2):
-                planes = psum.tile([P, PACK // 2, UNIT_TILES, P], F32, tag="planes")
-                for t2 in range(PACK // 2):
-                    t = half * (PACK // 2) + t2
-                    for i in range(UNIT_TILES):
-                        nc.tensor.transpose(
-                            planes[:, t2, i, :], live["normed", u][:, i, t * P : (t + 1) * P], ident_f32[:]
-                        )
-                live["planes", u, half] = planes
+        def transpose_normed(u, half):
+            planes = psum.tile([P, PACK // 2, UNIT_TILES, P], F32, tag="planes")
+            for t2 in range(PACK // 2):
+                t = half * (PACK // 2) + t2
+                for i in range(UNIT_TILES):
+                    nc.tensor.transpose(
+                        planes[:, t2, i, :], live["normed", u][:, i, t * P : (t + 1) * P], ident_f32[:]
+                    )
+            live["planes", u, half] = planes
 
         def gain_and_bias(u):
             h_planes = work.tile([P, PACK, UNIT_TOKENS], BF16)
@@ -287,19 +288,19 @@ def tile_swidtblock_pb_t_kernel(
             live["h_codes", u] = h_codes
             live["h_scales", u] = h_scales
 
-        def expand(u):
-            acc2 = psum.tile([P, UNIT_TILES, F], F32, tag="acc2")
-            for i in range(UNIT_TILES):
-                nc.tensor.matmul_mx(
-                    out=acc2[:, i, :],
-                    lhsT=live["h_codes", u][:, i * P : (i + 1) * P].bitcast(FP8X4),
-                    lhsT_scale=live["h_scales", u][:, i * P : (i + 1) * P],
-                    rhs=w1_codes[:].bitcast(FP8X4),
-                    rhs_scale=w1_scales[:],
-                    start=True,
-                    stop=True,
-                )
-            live["acc2", u] = acc2
+        def expand(u, i):
+            if i == 0:
+                acc2 = psum.tile([P, UNIT_TILES, F], F32, tag="acc2")
+                live["acc2", u] = acc2
+            nc.tensor.matmul_mx(
+                out=live["acc2", u][:, i, :],
+                lhsT=live["h_codes", u][:, i * P : (i + 1) * P].bitcast(FP8X4),
+                lhsT_scale=live["h_scales", u][:, i * P : (i + 1) * P],
+                rhs=w1_codes[:].bitcast(FP8X4),
+                rhs_scale=w1_scales[:],
+                start=True,
+                stop=True,
+            )
 
         def add_b1(u):
             pre_gelu = work.tile([P, UNIT_TILES, F], F32)
@@ -316,18 +317,19 @@ def tile_swidtblock_pb_t_kernel(
             nc.scalar.activation(out=g_sb[:], in_=live["pre_gelu", u][:], func=ACT.Gelu_apprx_tanh)
             nc.sync.dma_start(out=g_units[u], in_=g_sb[:])
 
-        def when_valid(stage, u):
+        def when_valid(stage, u, *part):
             if 0 <= u < UNITS:
-                stage(u)
+                stage(u, *part)
 
         with tc.manual_schedule():
             for slot in range(-2, UNITS + 7):
                 if slot >= 0:
                     when_valid(load, slot + INPUT_BUFS)
-                when_valid(project, slot)
-                when_valid(expand, slot - 5)
-                when_valid(transpose_normed, slot - 3)
-                when_valid(transpose_attn, slot + 2)
+                for i in range(UNIT_TILES):
+                    when_valid(project, slot, i)
+                    when_valid(expand, slot - 5, i)
+                    when_valid(transpose_normed, slot - 3, i)
+                    when_valid(transpose_attn, slot + 2, i)
                 when_valid(normalise_tile_0, slot - 2)
                 when_valid(group_h, slot - 4)
                 when_valid(add_bias_to_residual, slot + 1)

@@ -20,9 +20,9 @@ D = 512
 F = 256
 EPS = 1e-6
 PASSES = A // K_PASS
-UNIT_TILES = 2
-UNIT_TOKENS = UNIT_TILES * P
-UNITS = TOKENS // UNIT_TOKENS
+UNIT_TILES = [1] + [2] * 15 + [1]
+UNITS = len(UNIT_TILES)
+FIRST_TILE = [sum(UNIT_TILES[:u]) for u in range(UNITS)]
 INPUT_BUFS = 6
 RUN = 4
 
@@ -33,10 +33,10 @@ def tile_swidtblock_pb_t_kernel(
     tc, attn_out, residual, wo, bo, ln2_gain, ln2_bias, w1, b1, out_0, out_1
 ):
     nc = tc.nc
-    attn_units = attn_out.flatten_outer_dims().rearrange("(n p i) k -> n p (i k)", p=P, i=UNIT_TILES)
-    res_units = residual.flatten_outer_dims().rearrange("(n p i) d -> n p i d", p=P, i=UNIT_TILES)
-    x_units = out_0.flatten_outer_dims().rearrange("(n p i) d -> n p i d", p=P, i=UNIT_TILES)
-    g_units = out_1.flatten_outer_dims().rearrange("(n p i) f -> n p i f", p=P, i=UNIT_TILES)
+
+    def unit_rows(tensor, u):
+        rows = tensor.flatten_outer_dims()[FIRST_TILE[u] * P : (FIRST_TILE[u] + UNIT_TILES[u]) * P, :]
+        return rows.rearrange("(p i) c -> p i c", i=UNIT_TILES[u])
 
     with ExitStack() as ctx:
         const = ctx.enter_context(tc.tile_pool(name="const", bufs=1))
@@ -47,43 +47,50 @@ def tile_swidtblock_pb_t_kernel(
 
         live = {}
 
-        def load(u):
-            attn_sb = inputs.tile([P, UNIT_TILES * A], BF16)
-            nc.sync.dma_start(out=attn_sb[:], in_=attn_units[u])
-            res_sb = inputs.tile([P, UNIT_TILES, D], BF16)
-            nc.sync.dma_start(out=res_sb[:], in_=res_units[u])
+        def load_attn(u):
+            n = UNIT_TILES[u]
+            attn_sb = inputs.tile([P, n * A], BF16)
+            nc.sync.dma_start(out=attn_sb[:].rearrange("p (i k) -> p i k", i=n), in_=unit_rows(attn_out, u))
             live["attn_words", u] = attn_sb[:].bitcast(F32)
+
+        def load_residual(u):
+            res_sb = inputs.tile([P, UNIT_TILES[u], D], BF16)
+            nc.sync.dma_start(out=res_sb[:], in_=unit_rows(residual, u))
             live["res", u] = res_sb
 
         gelu_probe = const.tile([P, 1], F32)
         nc.vector.memset(gelu_probe[:], 0.0)
         bias_rows = const.tile([P, D + F], BF16)
         nc.vector.memset(bias_rows[:], 0.0)
-        norm_raw = const.tile([P, 2, 16], BF16)
-        nc.scalar.dma_start(out=norm_raw[:, 0, 0:PACK], in_=ln2_gain.rearrange("(p t) -> p t", t=PACK))
-        nc.scalar.dma_start(out=norm_raw[:, 1, 0:PACK], in_=ln2_bias.rearrange("(p t) -> p t", t=PACK))
-        w1_raw = const.tile([P, PACK, F], BF16)
-        nc.scalar.dma_start(out=w1_raw[:], in_=w1.rearrange("(p t) f -> p t f", t=PACK))
-        nc.scalar.dma_start(out=bias_rows[0:1, 0:D], in_=bo.rearrange("(o d) -> o d", o=1))
-        nc.scalar.dma_start(out=bias_rows[0:1, D : D + F], in_=b1.rearrange("(o f) -> o f", o=1))
+        ones = const.tile([P, P], BF16)
+        nc.vector.memset(ones[:], 1.0)
+        minus_half = const.tile([P, max(UNIT_TILES)], F32)
+        nc.vector.memset(minus_half[:], -0.5)
+        eps_col = const.tile([P, 1], F32)
+        nc.vector.memset(eps_col[:], EPS)
+        ident_f32 = const.tile([P, P], F32)
+        make_identity(nc, ident_f32[:])
         gelu_done = const.tile([P, 1], F32)
         nc.scalar.activation(out=gelu_done[:], in_=gelu_probe[:], func=ACT.Gelu_apprx_tanh)
 
+        load_attn(0)
         wo_raw = const.tile([P, PASSES, PACK, D], BF16)
         wo_rows = wo.rearrange("(s p t) c -> s p t c", s=PASSES, t=PACK)
         for s in range(PASSES):
             nc.sync.dma_start(out=wo_raw[:, s], in_=wo_rows[s])
-        for u in range(INPUT_BUFS):
-            load(u)
-
-        ident_f32 = const.tile([P, P], F32)
-        make_identity(nc, ident_f32[:])
-        ones = const.tile([P, P], BF16)
-        nc.vector.memset(ones[:], 1.0)
-        minus_half = const.tile([P, UNIT_TILES], F32)
-        nc.vector.memset(minus_half[:], -0.5)
-        eps_col = const.tile([P, 1], F32)
-        nc.vector.memset(eps_col[:], EPS)
+        nc.sync.dma_start(out=bias_rows[0:1, 0:D], in_=bo.rearrange("(o d) -> o d", o=1))
+        nc.sync.dma_start(out=bias_rows[0:1, D : D + F], in_=b1.rearrange("(o f) -> o f", o=1))
+        load_residual(0)
+        load_attn(1)
+        load_residual(1)
+        norm_raw = const.tile([P, 2, 16], BF16)
+        nc.sync.dma_start(out=norm_raw[:, 0, 0:PACK], in_=ln2_gain.rearrange("(p t) -> p t", t=PACK))
+        nc.sync.dma_start(out=norm_raw[:, 1, 0:PACK], in_=ln2_bias.rearrange("(p t) -> p t", t=PACK))
+        w1_raw = const.tile([P, PACK, F], BF16)
+        nc.sync.dma_start(out=w1_raw[:], in_=w1.rearrange("(p t) f -> p t f", t=PACK))
+        for u in range(2, INPUT_BUFS):
+            load_attn(u)
+            load_residual(u)
 
         def regroup(copy, grouped, planes):
             copy(
@@ -94,28 +101,38 @@ def tile_swidtblock_pb_t_kernel(
         wo_grouped = const.tile([P, PASSES, D * PACK], BF16, align_bytes=64)
         wo_codes = const.tile([P, PASSES, D], U32, align_bytes=64)
         wo_scales = const.tile([P, PASSES, D], U8, align_bytes=64)
-        for s in range(PASSES):
-            regroup(nc.vector.tensor_copy, wo_grouped[:, s, :], wo_raw[:, s])
-        for s in range(PASSES):
-            nc.vector.quantize_mx(
-                out=wo_codes[:, s, :].bitcast(FP8X4), scales=wo_scales[:, s, :], in_=wo_grouped[:, s, :]
-            )
         w1_grouped = const.tile([P, F * PACK], BF16, align_bytes=64)
         w1_codes = const.tile([P, F], U32, align_bytes=64)
         w1_scales = const.tile([P, F], U8, align_bytes=64)
-        regroup(nc.scalar.copy, w1_grouped[:], w1_raw[:])
-        nc.vector.quantize_mx(out=w1_codes[:].bitcast(FP8X4), scales=w1_scales[:], in_=w1_grouped[:])
 
-        bo_ps = psum.tile([P, D], F32, tag="acc")
-        nc.tensor.matmul(out=bo_ps[:], lhsT=ones[:], rhs=bias_rows[:, 0:D], start=True, stop=True)
+        def prepare_wo():
+            shared = 336
+            regroup(nc.vector.tensor_copy, wo_grouped[:, 0, :], wo_raw[:, 0])
+            regroup(nc.vector.tensor_copy, wo_grouped[:, 1, 0 : shared * PACK], wo_raw[:, 1, :, 0:shared])
+            regroup(nc.scalar.copy, wo_grouped[:, 1, shared * PACK :], wo_raw[:, 1, :, shared:])
+            for s in range(PASSES):
+                nc.vector.quantize_mx(
+                    out=wo_codes[:, s, :].bitcast(FP8X4), scales=wo_scales[:, s, :], in_=wo_grouped[:, s, :]
+                )
+
+        def regroup_w1():
+            regroup(nc.scalar.copy, w1_grouped[:], w1_raw[:])
+
+        def quantise_w1():
+            nc.vector.quantize_mx(out=w1_codes[:].bitcast(FP8X4), scales=w1_scales[:], in_=w1_grouped[:])
+
         bo_all = const.tile([P, D], F32)
-        nc.scalar.copy(out=bo_all[:], in_=bo_ps[:])
-        b1_ps = psum.tile([P, F], F32, tag="acc")
-        nc.tensor.matmul(out=b1_ps[:], lhsT=ones[:], rhs=bias_rows[:, D : D + F], start=True, stop=True)
         b1_all = const.tile([P, F], F32)
-        nc.scalar.copy(out=b1_all[:], in_=b1_ps[:])
         norm_cols = const.tile([P, 2 * PACK], F32)
-        nc.scalar.copy(out=norm_cols[:].rearrange("p (g t) -> p g t", g=2), in_=norm_raw[:, :, 0:PACK])
+
+        def spread_bias(spread, columns):
+            bias_ps = psum.tile([P, D], F32, tag="acc")
+            n = columns.stop - columns.start
+            nc.tensor.matmul(out=bias_ps[:, 0:n], lhsT=ones[:], rhs=bias_rows[:, columns], start=True, stop=True)
+            nc.scalar.copy(out=spread[:], in_=bias_ps[:, 0:n])
+
+        def norm_columns():
+            nc.scalar.copy(out=norm_cols[:].rearrange("p (g t) -> p g t", g=2), in_=norm_raw[:, :, 0:PACK])
 
         def transpose_attn(u, i):
             at = psum.tile([P, PASSES * 2, P], F32, tag="at")
@@ -130,19 +147,18 @@ def tile_swidtblock_pb_t_kernel(
             live["at", u, i] = at
 
         def group_attn(u):
-            a_grouped = work.tile([P, UNIT_TILES * PASSES * P * PACK], BF16, align_bytes=64)
-            words = a_grouped[:].bitcast(F32).rearrange(
-                "p (i s j u) -> p i s j u", i=UNIT_TILES, s=PASSES, u=2
-            )
-            for i in range(UNIT_TILES):
+            n = UNIT_TILES[u]
+            a_grouped = work.tile([P, n * PASSES * P * PACK], BF16, align_bytes=64)
+            words = a_grouped[:].bitcast(F32).rearrange("p (i s j u) -> p i s j u", i=n, s=PASSES, u=2)
+            for i in range(n):
                 nc.scalar.copy(
                     out=words[:, i], in_=live["at", u, i][:].rearrange("p (s u) j -> p s j u", u=2)
                 )
             live["a_grouped", u] = a_grouped
 
         def quantise_attn(u):
-            a_codes = work.tile([P, UNIT_TILES, PASSES, P], U32, align_bytes=64)
-            a_scales = work.tile([P, UNIT_TILES, PASSES, P], U8, align_bytes=64)
+            a_codes = work.tile([P, UNIT_TILES[u], PASSES, P], U32, align_bytes=64)
+            a_scales = work.tile([P, UNIT_TILES[u], PASSES, P], U8, align_bytes=64)
             nc.vector.quantize_mx(
                 out=a_codes[:].rearrange("p i s j -> p (i s j)").bitcast(FP8X4),
                 scales=a_scales[:].rearrange("p i s j -> p (i s j)"),
@@ -166,19 +182,21 @@ def tile_swidtblock_pb_t_kernel(
             live["acc", u, i] = acc
 
         def add_bias_to_residual(u):
-            res_bo = held.tile([P, UNIT_TILES, D], F32)
+            n = UNIT_TILES[u]
+            res_bo = held.tile([P, n, D], F32)
             nc.vector.tensor_tensor(
                 out=res_bo[:],
                 in0=live["res", u][:],
-                in1=bo_all[:].unsqueeze(1).to_broadcast([P, UNIT_TILES, D]),
+                in1=bo_all[:].unsqueeze(1).to_broadcast([P, n, D]),
                 op=ALU.add,
             )
             live["res_bo", u] = res_bo
 
         def finish_x_mid(u):
-            x_mid = held.tile([P, UNIT_TILES, D], F32)
-            row_sum = held.tile([P, UNIT_TILES], F32)
-            for i in range(UNIT_TILES):
+            n = UNIT_TILES[u]
+            x_mid = held.tile([P, n, D], F32)
+            row_sum = held.tile([P, n], F32)
+            for i in range(n):
                 nc.vector.scalar_tensor_tensor(
                     out=x_mid[:, i, :],
                     in0=live["acc", u, i][:],
@@ -188,18 +206,18 @@ def tile_swidtblock_pb_t_kernel(
                     op1=ALU.add,
                     accum_out=row_sum[:, i : i + 1],
                 )
-            nc.sync.dma_start(out=x_units[u], in_=x_mid[:])
+            nc.sync.dma_start(out=unit_rows(out_0, u), in_=x_mid[:])
             live["x_mid", u] = x_mid
             live["row_sum", u] = row_sum
 
         def negate_mean(u):
-            neg_mean = held.tile([P, UNIT_TILES], F32)
+            neg_mean = held.tile([P, UNIT_TILES[u]], F32)
             nc.scalar.mul(out=neg_mean[:], in_=live["row_sum", u][:], mul=-1.0 / D)
             live["neg_mean", u] = neg_mean
 
         def sum_squares(u):
-            sq_sum = held.tile([P, UNIT_TILES], F32)
-            for i in range(UNIT_TILES):
+            sq_sum = held.tile([P, UNIT_TILES[u]], F32)
+            for i in range(UNIT_TILES[u]):
                 squares = work.tile([P, D], BF16)
                 nc.scalar.activation(
                     out=squares[:],
@@ -212,12 +230,13 @@ def tile_swidtblock_pb_t_kernel(
             live["sq_sum", u] = sq_sum
 
         def inverse_std(u):
-            var_eps = held.tile([P, UNIT_TILES], F32)
+            n = UNIT_TILES[u]
+            var_eps = held.tile([P, n], F32)
             nc.scalar.activation(
                 out=var_eps[:], in_=live["sq_sum", u][:], func=ACT.Identity, scale=1.0 / D, bias=eps_col[:]
             )
-            rstd = held.tile([P, UNIT_TILES], F32)
-            nc.gpsimd.tensor_tensor(out=rstd[:], in0=var_eps[:], in1=minus_half[:], op=ALU.pow)
+            rstd = held.tile([P, n], F32)
+            nc.gpsimd.tensor_tensor(out=rstd[:], in0=var_eps[:], in1=minus_half[:, 0:n], op=ALU.pow)
             live["rstd", u] = rstd
 
         def by_plane(rows):
@@ -227,7 +246,7 @@ def tile_swidtblock_pb_t_kernel(
             return rows.rearrange("p (t c i) -> p c t i", i=RUN, t=PACK)
 
         def normalise_tile_0(u):
-            normed = work.tile([P, UNIT_TILES, D], F32)
+            normed = work.tile([P, UNIT_TILES[u], D], F32)
             nc.vector.tensor_scalar(
                 out=planes_of(normed[:, 0, :]),
                 in0=by_plane(live["x_mid", u][:, 0, :]),
@@ -239,6 +258,8 @@ def tile_swidtblock_pb_t_kernel(
             live["normed", u] = normed
 
         def shift_of_tile_1(u):
+            if UNIT_TILES[u] == 1:
+                return
             shift = held.tile([P, 1], F32)
             nc.scalar.activation(
                 out=shift[:], in_=live["neg_mean", u][:, 1:2], func=ACT.Identity, scale=live["rstd", u][:, 1:2]
@@ -246,6 +267,8 @@ def tile_swidtblock_pb_t_kernel(
             live["shift", u] = shift
 
         def normalise_tile_1(u):
+            if UNIT_TILES[u] == 1:
+                return
             nc.scalar.activation(
                 out=planes_of(live["normed", u][:, 1, :]),
                 in_=by_plane(live["x_mid", u][:, 1, :]),
@@ -255,17 +278,17 @@ def tile_swidtblock_pb_t_kernel(
             )
 
         def transpose_normed(u, half):
-            planes = psum.tile([P, PACK // 2, UNIT_TILES, P], F32, tag="planes")
+            planes = psum.tile([P, PACK // 2, UNIT_TILES[u], P], F32, tag="planes")
             for t2 in range(PACK // 2):
                 t = half * (PACK // 2) + t2
-                for i in range(UNIT_TILES):
+                for i in range(UNIT_TILES[u]):
                     nc.tensor.transpose(
                         planes[:, t2, i, :], live["normed", u][:, i, t * P : (t + 1) * P], ident_f32[:]
                     )
             live["planes", u, half] = planes
 
         def gain_and_bias(u):
-            h_planes = work.tile([P, PACK, UNIT_TOKENS], BF16)
+            h_planes = work.tile([P, PACK, UNIT_TILES[u] * P], BF16)
             for t in range(PACK):
                 nc.scalar.activation(
                     out=h_planes[:, t, :],
@@ -277,20 +300,20 @@ def tile_swidtblock_pb_t_kernel(
             live["h_planes", u] = h_planes
 
         def group_h(u):
-            h_grouped = work.tile([P, UNIT_TOKENS * PACK], BF16, align_bytes=64)
+            h_grouped = work.tile([P, UNIT_TILES[u] * P * PACK], BF16, align_bytes=64)
             regroup(nc.vector.tensor_copy, h_grouped[:], live["h_planes", u][:])
             live["h_grouped", u] = h_grouped
 
         def quantise_h(u):
-            h_codes = work.tile([P, UNIT_TOKENS], U32, align_bytes=64)
-            h_scales = work.tile([P, UNIT_TOKENS], U8, align_bytes=64)
+            h_codes = work.tile([P, UNIT_TILES[u] * P], U32, align_bytes=64)
+            h_scales = work.tile([P, UNIT_TILES[u] * P], U8, align_bytes=64)
             nc.vector.quantize_mx(out=h_codes[:].bitcast(FP8X4), scales=h_scales[:], in_=live["h_grouped", u][:])
             live["h_codes", u] = h_codes
             live["h_scales", u] = h_scales
 
         def expand(u, i):
             if i == 0:
-                acc2 = psum.tile([P, UNIT_TILES, F], F32, tag="acc2")
+                acc2 = psum.tile([P, UNIT_TILES[u], F], F32, tag="acc2")
                 live["acc2", u] = acc2
             nc.tensor.matmul_mx(
                 out=live["acc2", u][:, i, :],
@@ -303,36 +326,51 @@ def tile_swidtblock_pb_t_kernel(
             )
 
         def add_b1(u):
-            pre_gelu = work.tile([P, UNIT_TILES, F], F32)
+            n = UNIT_TILES[u]
+            pre_gelu = work.tile([P, n, F], F32)
             nc.vector.tensor_tensor(
                 out=pre_gelu[:],
                 in0=live["acc2", u][:],
-                in1=b1_all[:].unsqueeze(1).to_broadcast([P, UNIT_TILES, F]),
+                in1=b1_all[:].unsqueeze(1).to_broadcast([P, n, F]),
                 op=ALU.add,
             )
             live["pre_gelu", u] = pre_gelu
 
         def gelu_and_store(u):
-            g_sb = held.tile([P, UNIT_TILES, F], F32)
+            g_sb = held.tile([P, UNIT_TILES[u], F], F32)
             nc.scalar.activation(out=g_sb[:], in_=live["pre_gelu", u][:], func=ACT.Gelu_apprx_tanh)
-            nc.sync.dma_start(out=g_units[u], in_=g_sb[:])
+            nc.sync.dma_start(out=unit_rows(out_1, u), in_=g_sb[:])
 
         def when_valid(stage, u, *part):
             if 0 <= u < UNITS:
                 stage(u, *part)
 
+        def for_tile(stage, u, i):
+            if 0 <= u < UNITS and i < UNIT_TILES[u]:
+                stage(u, i)
+
         with tc.manual_schedule():
             for slot in range(-2, UNITS + 7):
                 if slot >= 0:
-                    when_valid(load, slot + INPUT_BUFS)
-                for i in range(UNIT_TILES):
-                    when_valid(project, slot, i)
-                    when_valid(expand, slot - 5, i)
-                    when_valid(transpose_normed, slot - 3, i)
-                    when_valid(transpose_attn, slot + 2, i)
-                when_valid(normalise_tile_0, slot - 2)
+                    when_valid(load_attn, slot + INPUT_BUFS)
+                    when_valid(load_residual, slot + INPUT_BUFS)
+                if slot == -1:
+                    prepare_wo()
+                    spread_bias(bo_all, slice(0, D))
+                if slot == 0:
+                    spread_bias(b1_all, slice(D, D + F))
+                    norm_columns()
+                    regroup_w1()
+                if slot == 1:
+                    quantise_w1()
+                for half in range(2):
+                    for_tile(project, slot, half)
+                    for_tile(expand, slot - 5, half)
+                    when_valid(transpose_normed, slot - 3, half)
+                    for_tile(transpose_attn, slot + 2, half)
                 when_valid(group_h, slot - 4)
                 when_valid(add_bias_to_residual, slot + 1)
+                when_valid(normalise_tile_0, slot - 2)
                 when_valid(quantise_h, slot - 4)
                 when_valid(quantise_attn, slot + 1)
                 when_valid(finish_x_mid, slot)

@@ -24,6 +24,7 @@ UNIT_TILES = [1] + [2] * 15 + [1]
 UNITS = len(UNIT_TILES)
 FIRST_TILE = [sum(UNIT_TILES[:u]) for u in range(UNITS)]
 INPUT_BUFS = 6
+Q = 8
 RUN = 4
 
 FLOPS = 2 * TOKENS * A * D + 2 * TOKENS * D * F
@@ -70,6 +71,10 @@ def tile_swidtblock_pb_t_kernel(
         nc.vector.memset(eps_col[:], EPS)
         ident_f32 = const.tile([P, P], F32)
         make_identity(nc, ident_f32[:])
+        ident_bf16 = const.tile([P, P], BF16)
+        make_identity(nc, ident_bf16[:])
+        norm_rows = const.tile([P, P], BF16)
+        nc.vector.memset(norm_rows[:], 0.0)
         gelu_done = const.tile([P, 1], F32)
         nc.scalar.activation(out=gelu_done[:], in_=gelu_probe[:], func=ACT.Gelu_apprx_tanh)
 
@@ -83,11 +88,15 @@ def tile_swidtblock_pb_t_kernel(
         load_residual(0)
         load_attn(1)
         load_residual(1)
-        norm_raw = const.tile([P, 2, 16], BF16)
-        nc.sync.dma_start(out=norm_raw[:, 0, 0:PACK], in_=ln2_gain.rearrange("(p t) -> p t", t=PACK))
-        nc.sync.dma_start(out=norm_raw[:, 1, 0:PACK], in_=ln2_bias.rearrange("(p t) -> p t", t=PACK))
+        for row, vector in ((0, ln2_gain), (PACK, ln2_bias)):
+            nc.sync.dma_start(
+                out=norm_rows[row : row + PACK, :].rearrange("t (b q) -> t b q", q=Q),
+                in_=vector.rearrange("(b t q) -> t b q", t=PACK, q=Q),
+            )
         w1_raw = const.tile([P, PACK, F], BF16)
-        nc.sync.dma_start(out=w1_raw[:], in_=w1.rearrange("(p t) f -> p t f", t=PACK))
+        w1_rows = w1.rearrange("(b t q) f -> t b q f", t=PACK, q=Q)
+        for t in range(PACK):
+            nc.sync.dma_start(out=w1_raw[:, t, :], in_=w1_rows[t])
         for u in range(2, INPUT_BUFS):
             load_attn(u)
             load_residual(u)
@@ -132,7 +141,9 @@ def tile_swidtblock_pb_t_kernel(
             nc.scalar.copy(out=spread[:], in_=bias_ps[:, 0:n])
 
         def norm_columns():
-            nc.scalar.copy(out=norm_cols[:].rearrange("p (g t) -> p g t", g=2), in_=norm_raw[:, :, 0:PACK])
+            norm_ps = psum.tile([P, P], BF16, tag="planes")
+            nc.tensor.transpose(norm_ps[:], norm_rows[:], ident_bf16[:])
+            nc.scalar.copy(out=norm_cols[:], in_=norm_ps[:, 0 : 2 * PACK])
 
         def transpose_attn(u, i):
             at = psum.tile([P, PASSES * 2, P], F32, tag="at")
@@ -240,25 +251,29 @@ def tile_swidtblock_pb_t_kernel(
             live["rstd", u] = rstd
 
         def by_plane(rows):
-            return rows.rearrange("p (c i t) -> p c t i", i=RUN, t=PACK)
+            return rows.rearrange("p (b t q) -> p t b q", t=PACK, q=Q)
 
         def planes_of(rows):
-            return rows.rearrange("p (t c i) -> p c t i", i=RUN, t=PACK)
+            return rows.rearrange("p (t b q) -> p t b q", t=PACK, q=Q)
 
-        def normalise_tile_0(u):
+        def scalar_normalises(u):
+            return UNIT_TILES[u] == 2 and u < UNITS - 3
+
+        def normalise_on_vector(u):
             normed = work.tile([P, UNIT_TILES[u], D], F32)
-            nc.vector.tensor_scalar(
-                out=planes_of(normed[:, 0, :]),
-                in0=by_plane(live["x_mid", u][:, 0, :]),
-                scalar1=live["neg_mean", u][:, 0:1],
-                scalar2=live["rstd", u][:, 0:1],
-                op0=ALU.add,
-                op1=ALU.mult,
-            )
+            for i in range(1 if scalar_normalises(u) else UNIT_TILES[u]):
+                nc.vector.tensor_scalar(
+                    out=planes_of(normed[:, i, :]),
+                    in0=by_plane(live["x_mid", u][:, i, :]),
+                    scalar1=live["neg_mean", u][:, i : i + 1],
+                    scalar2=live["rstd", u][:, i : i + 1],
+                    op0=ALU.add,
+                    op1=ALU.mult,
+                )
             live["normed", u] = normed
 
         def shift_of_tile_1(u):
-            if UNIT_TILES[u] == 1:
+            if not scalar_normalises(u):
                 return
             shift = held.tile([P, 1], F32)
             nc.scalar.activation(
@@ -266,8 +281,8 @@ def tile_swidtblock_pb_t_kernel(
             )
             live["shift", u] = shift
 
-        def normalise_tile_1(u):
-            if UNIT_TILES[u] == 1:
+        def normalise_on_scalar(u):
+            if not scalar_normalises(u):
                 return
             nc.scalar.activation(
                 out=planes_of(live["normed", u][:, 1, :]),
@@ -370,7 +385,7 @@ def tile_swidtblock_pb_t_kernel(
                     for_tile(transpose_attn, slot + 2, half)
                 when_valid(group_h, slot - 4)
                 when_valid(add_bias_to_residual, slot + 1)
-                when_valid(normalise_tile_0, slot - 2)
+                when_valid(normalise_on_vector, slot - 2)
                 when_valid(quantise_h, slot - 4)
                 when_valid(quantise_attn, slot + 1)
                 when_valid(finish_x_mid, slot)
@@ -379,7 +394,7 @@ def tile_swidtblock_pb_t_kernel(
                 when_valid(shift_of_tile_1, slot - 2)
                 when_valid(gelu_and_store, slot - 6)
                 when_valid(sum_squares, slot - 1)
-                when_valid(normalise_tile_1, slot - 2)
+                when_valid(normalise_on_scalar, slot - 2)
                 when_valid(inverse_std, slot - 1)
                 when_valid(gain_and_bias, slot - 3)
                 when_valid(group_attn, slot + 2)

@@ -43,7 +43,7 @@ def tile_swidtblock_pb_t_kernel(
         const = ctx.enter_context(tc.tile_pool(name="const", bufs=1))
         inputs = ctx.enter_context(tc.tile_pool(name="inputs", bufs=INPUT_BUFS))
         work = ctx.enter_context(tc.tile_pool(name="work", bufs=2))
-        held = ctx.enter_context(tc.tile_pool(name="held", bufs=3))
+        held = ctx.enter_context(tc.tile_pool(name="held", bufs=4))
         psum = ctx.enter_context(tc.psum_pool(name="psum", bufs=2))
 
         live = {}
@@ -193,15 +193,19 @@ def tile_swidtblock_pb_t_kernel(
             live["acc", u, i] = acc
 
         def add_bias_to_residual(u):
-            n = UNIT_TILES[u]
-            res_bo = held.tile([P, n, D], F32)
-            nc.vector.tensor_tensor(
-                out=res_bo[:],
-                in0=live["res", u][:],
-                in1=bo_all[:].unsqueeze(1).to_broadcast([P, n, D]),
-                op=ALU.add,
-            )
+            res_bo = held.tile([P, UNIT_TILES[u], D], F32)
+            nc.vector.tensor_tensor(out=res_bo[:, 0, :], in0=live["res", u][:, 0, :], in1=bo_all[:], op=ALU.add)
             live["res_bo", u] = res_bo
+
+        def release_gpsimd(u):
+            if UNIT_TILES[u] == 2:
+                nc.vector.memset(live["res_bo", u][:, 1, 0:1], 0.0)
+
+        def add_bias_on_gpsimd(u):
+            if UNIT_TILES[u] == 2:
+                nc.gpsimd.tensor_tensor(
+                    out=live["res_bo", u][:, 1, :], in0=live["res", u][:, 1, :], in1=bo_all[:], op=ALU.add
+                )
 
         def finish_x_mid(u):
             n = UNIT_TILES[u]
@@ -257,7 +261,7 @@ def tile_swidtblock_pb_t_kernel(
             return rows.rearrange("p (t b q) -> p t b q", t=PACK, q=Q)
 
         def scalar_normalises(u):
-            return UNIT_TILES[u] == 2 and u < UNITS - 3
+            return UNIT_TILES[u] == 2 and u % 2 > 0 and u < UNITS - 3
 
         def normalise_on_vector(u):
             normed = work.tile([P, UNIT_TILES[u], D], F32)
@@ -369,7 +373,7 @@ def tile_swidtblock_pb_t_kernel(
                 if slot >= 0:
                     when_valid(load_attn, slot + INPUT_BUFS)
                     when_valid(load_residual, slot + INPUT_BUFS)
-                if slot == -1:
+                if slot == -2:
                     prepare_wo()
                     spread_bias(bo_all, slice(0, D))
                 if slot == 0:
@@ -384,15 +388,17 @@ def tile_swidtblock_pb_t_kernel(
                     when_valid(transpose_normed, slot - 3, half)
                     for_tile(transpose_attn, slot + 2, half)
                 when_valid(group_h, slot - 4)
-                when_valid(add_bias_to_residual, slot + 1)
+                when_valid(add_bias_to_residual, slot + 2)
                 when_valid(normalise_on_vector, slot - 2)
                 when_valid(quantise_h, slot - 4)
                 when_valid(quantise_attn, slot + 1)
+                when_valid(release_gpsimd, slot + 2)
+                when_valid(add_bias_on_gpsimd, slot + 2)
                 when_valid(finish_x_mid, slot)
                 when_valid(add_b1, slot - 5)
                 when_valid(negate_mean, slot - 1)
-                when_valid(shift_of_tile_1, slot - 2)
                 when_valid(gelu_and_store, slot - 6)
+                when_valid(shift_of_tile_1, slot - 2)
                 when_valid(sum_squares, slot - 1)
                 when_valid(normalise_on_scalar, slot - 2)
                 when_valid(inverse_std, slot - 1)

@@ -43,7 +43,7 @@ def tile_swidtblock_pb_t_kernel(
         const = ctx.enter_context(tc.tile_pool(name="const", bufs=1))
         inputs = ctx.enter_context(tc.tile_pool(name="inputs", bufs=INPUT_BUFS))
         work = ctx.enter_context(tc.tile_pool(name="work", bufs=2))
-        held = ctx.enter_context(tc.tile_pool(name="held", bufs=4))
+        held = ctx.enter_context(tc.tile_pool(name="held", bufs=3))
         psum = ctx.enter_context(tc.psum_pool(name="psum", bufs=2))
 
         live = {}
@@ -78,11 +78,11 @@ def tile_swidtblock_pb_t_kernel(
         gelu_done = const.tile([P, 1], F32)
         nc.scalar.activation(out=gelu_done[:], in_=gelu_probe[:], func=ACT.Gelu_apprx_tanh)
 
-        load_attn(0)
         wo_raw = const.tile([P, PASSES, PACK, D], BF16)
         wo_rows = wo.rearrange("(s p t) c -> s p t c", s=PASSES, t=PACK)
-        for s in range(PASSES):
-            nc.sync.dma_start(out=wo_raw[:, s], in_=wo_rows[s])
+        nc.sync.dma_start(out=wo_raw[:, 0], in_=wo_rows[0])
+        load_attn(0)
+        nc.sync.dma_start(out=wo_raw[:, 1], in_=wo_rows[1])
         nc.sync.dma_start(out=bias_rows[0:1, 0:D], in_=bo.rearrange("(o d) -> o d", o=1))
         nc.sync.dma_start(out=bias_rows[0:1, D : D + F], in_=b1.rearrange("(o f) -> o f", o=1))
         load_residual(0)
@@ -306,17 +306,18 @@ def tile_swidtblock_pb_t_kernel(
                     )
             live["planes", u, half] = planes
 
-        def gain_and_bias(u):
-            h_planes = work.tile([P, PACK, UNIT_TILES[u] * P], BF16)
-            for t in range(PACK):
+        def gain_and_bias(u, half):
+            if half == 0:
+                h_planes = work.tile([P, PACK, UNIT_TILES[u] * P], BF16)
+                live["h_planes", u] = h_planes
+            for t in range(half * PACK // 2, (half + 1) * PACK // 2):
                 nc.scalar.activation(
-                    out=h_planes[:, t, :],
-                    in_=live["planes", u, t // (PACK // 2)][:, t % (PACK // 2)].rearrange("p i j -> p (i j)"),
+                    out=live["h_planes", u][:, t, :],
+                    in_=live["planes", u, half][:, t % (PACK // 2)].rearrange("p i j -> p (i j)"),
                     func=ACT.Identity,
                     scale=norm_cols[:, t : t + 1],
                     bias=norm_cols[:, PACK + t : PACK + t + 1],
                 )
-            live["h_planes", u] = h_planes
 
         def group_h(u):
             h_grouped = work.tile([P, UNIT_TILES[u] * P * PACK], BF16, align_bytes=64)
@@ -373,7 +374,7 @@ def tile_swidtblock_pb_t_kernel(
                 if slot >= 0:
                     when_valid(load_attn, slot + INPUT_BUFS)
                     when_valid(load_residual, slot + INPUT_BUFS)
-                if slot == -2:
+                if slot == -1:
                     prepare_wo()
                     spread_bias(bo_all, slice(0, D))
                 if slot == 0:
@@ -388,19 +389,20 @@ def tile_swidtblock_pb_t_kernel(
                     when_valid(transpose_normed, slot - 3, half)
                     for_tile(transpose_attn, slot + 2, half)
                 when_valid(group_h, slot - 4)
-                when_valid(add_bias_to_residual, slot + 2)
-                when_valid(normalise_on_vector, slot - 2)
+                when_valid(add_bias_to_residual, slot + 1)
                 when_valid(quantise_h, slot - 4)
+                when_valid(normalise_on_vector, slot - 2)
                 when_valid(quantise_attn, slot + 1)
-                when_valid(release_gpsimd, slot + 2)
-                when_valid(add_bias_on_gpsimd, slot + 2)
+                when_valid(release_gpsimd, slot + 1)
+                when_valid(add_bias_on_gpsimd, slot + 1)
                 when_valid(finish_x_mid, slot)
                 when_valid(add_b1, slot - 5)
                 when_valid(negate_mean, slot - 1)
                 when_valid(gelu_and_store, slot - 6)
-                when_valid(shift_of_tile_1, slot - 2)
                 when_valid(sum_squares, slot - 1)
-                when_valid(normalise_on_scalar, slot - 2)
+                when_valid(shift_of_tile_1, slot - 2)
+                when_valid(gain_and_bias, slot - 3, 0)
                 when_valid(inverse_std, slot - 1)
-                when_valid(gain_and_bias, slot - 3)
+                when_valid(normalise_on_scalar, slot - 2)
+                when_valid(gain_and_bias, slot - 3, 1)
                 when_valid(group_attn, slot + 2)

@@ -383,26 +383,28 @@ def tile_swidtblock_pb_t_kernel(
                     regroup_w1()
                 if slot == 1:
                     quantise_w1()
+                for stage, u in ((project, slot), (expand, slot - 5)):
+                    for_tile(stage, u, 0)
+                    for_tile(stage, u, 1)
                 for half in range(2):
-                    for_tile(project, slot, half)
-                    for_tile(expand, slot - 5, half)
                     when_valid(transpose_normed, slot - 3, half)
+                for half in range(2):
                     for_tile(transpose_attn, slot + 2, half)
                 when_valid(group_h, slot - 4)
                 when_valid(add_bias_to_residual, slot + 1)
-                when_valid(quantise_h, slot - 4)
-                when_valid(normalise_on_vector, slot - 2)
-                when_valid(quantise_attn, slot + 1)
                 when_valid(release_gpsimd, slot + 1)
                 when_valid(add_bias_on_gpsimd, slot + 1)
                 when_valid(finish_x_mid, slot)
+                when_valid(quantise_attn, slot + 1)
+                when_valid(quantise_h, slot - 4)
+                when_valid(normalise_on_vector, slot - 2)
                 when_valid(add_b1, slot - 5)
-                when_valid(negate_mean, slot - 1)
-                when_valid(gelu_and_store, slot - 6)
                 when_valid(sum_squares, slot - 1)
+                when_valid(gelu_and_store, slot - 6)
+                when_valid(inverse_std, slot - 1)
                 when_valid(shift_of_tile_1, slot - 2)
                 when_valid(gain_and_bias, slot - 3, 0)
-                when_valid(inverse_std, slot - 1)
                 when_valid(normalise_on_scalar, slot - 2)
                 when_valid(gain_and_bias, slot - 3, 1)
                 when_valid(group_attn, slot + 2)
+                when_valid(negate_mean, slot)

@@ -192,14 +192,16 @@ def tile_swidtblock_pb_t_kernel(
                 )
             live["acc", u, i] = acc
 
-        def add_bias_to_residual(u):
-            res_bo = held.tile([P, UNIT_TILES[u], D], F32)
-            nc.vector.tensor_tensor(out=res_bo[:, 0, :], in0=live["res", u][:, 0, :], in1=bo_all[:], op=ALU.add)
-            live["res_bo", u] = res_bo
-
         def release_gpsimd(u):
+            res_bo = held.tile([P, UNIT_TILES[u], D], F32)
+            live["res_bo", u] = res_bo
             if UNIT_TILES[u] == 2:
-                nc.vector.memset(live["res_bo", u][:, 1, 0:1], 0.0)
+                nc.vector.memset(res_bo[:, 1, 0:1], 0.0)
+
+        def add_bias_to_residual(u):
+            nc.vector.tensor_tensor(
+                out=live["res_bo", u][:, 0, :], in0=live["res", u][:, 0, :], in1=bo_all[:], op=ALU.add
+            )
 
         def add_bias_on_gpsimd(u):
             if UNIT_TILES[u] == 2:
@@ -391,8 +393,8 @@ def tile_swidtblock_pb_t_kernel(
                 for half in range(2):
                     for_tile(transpose_attn, slot + 2, half)
                 when_valid(group_h, slot - 4)
-                when_valid(add_bias_to_residual, slot + 1)
                 when_valid(release_gpsimd, slot + 1)
+                when_valid(add_bias_to_residual, slot + 1)
                 when_valid(add_bias_on_gpsimd, slot + 1)
                 when_valid(finish_x_mid, slot)
                 when_valid(quantise_attn, slot + 1)
@@ -406,5 +408,5 @@ def tile_swidtblock_pb_t_kernel(
                 when_valid(gain_and_bias, slot - 3, 0)
                 when_valid(normalise_on_scalar, slot - 2)
                 when_valid(gain_and_bias, slot - 3, 1)
-                when_valid(group_attn, slot + 2)
                 when_valid(negate_mean, slot)
+                when_valid(group_attn, slot + 2)

from contextlib import ExitStack

import concourse.mybir as mybir
from concourse.masks import make_identity

F32 = mybir.dt.float32
BF16 = mybir.dt.bfloat16
U32 = mybir.dt.uint32
U8 = mybir.dt.uint8
FP8X4 = mybir.dt.float8_e4m3fn_x4
ALU = mybir.AluOpType
ACT = mybir.ActivationFunctionType

P = 128
PACK = 4
K_PASS = P * PACK
TOKENS = 4 * 1024
A = 1024
D = 512
F = 256
EPS = 1e-6
PASSES = A // K_PASS
UNIT_TILES = [1] + [2] * 15 + [1]
UNITS = len(UNIT_TILES)
FIRST_TILE = [sum(UNIT_TILES[:u]) for u in range(UNITS)]
INPUT_BUFS = 6
Q = 8
RUN = 4

FLOPS = 2 * TOKENS * A * D + 2 * TOKENS * D * F


def tile_swidtblock_pb_t_kernel(
    tc, attn_out, residual, wo, bo, ln2_gain, ln2_bias, w1, b1, out_0, out_1
):
    nc = tc.nc

    def unit_rows(tensor, u):
        rows = tensor.flatten_outer_dims()[FIRST_TILE[u] * P : (FIRST_TILE[u] + UNIT_TILES[u]) * P, :]
        return rows.rearrange("(p i) c -> p i c", i=UNIT_TILES[u])

    with ExitStack() as ctx:
        const = ctx.enter_context(tc.tile_pool(name="const", bufs=1))
        inputs = ctx.enter_context(tc.tile_pool(name="inputs", bufs=INPUT_BUFS))
        work = ctx.enter_context(tc.tile_pool(name="work", bufs=2))
        held = ctx.enter_context(tc.tile_pool(name="held", bufs=3))
        psum = ctx.enter_context(tc.psum_pool(name="psum", bufs=2))

        live = {}

        def load_attn(u):
            n = UNIT_TILES[u]
            attn_sb = inputs.tile([P, n * A], BF16)
            nc.sync.dma_start(out=attn_sb[:].rearrange("p (i k) -> p i k", i=n), in_=unit_rows(attn_out, u))
            live["attn_words", u] = attn_sb[:].bitcast(F32)

        def load_residual(u):
            res_sb = inputs.tile([P, UNIT_TILES[u], D], BF16)
            nc.sync.dma_start(out=res_sb[:], in_=unit_rows(residual, u))
            live["res", u] = res_sb

        gelu_probe = const.tile([P, 1], F32)
        nc.vector.memset(gelu_probe[:], 0.0)
        bias_rows = const.tile([P, D + F], BF16)
        nc.vector.memset(bias_rows[:], 0.0)
        ones = const.tile([P, P], BF16)
        nc.vector.memset(ones[:], 1.0)
        minus_half = const.tile([P, max(UNIT_TILES)], F32)
        nc.vector.memset(minus_half[:], -0.5)
        eps_col = const.tile([P, 1], F32)
        nc.vector.memset(eps_col[:], EPS)
        ident_f32 = const.tile([P, P], F32)
        make_identity(nc, ident_f32[:])
        ident_bf16 = const.tile([P, P], BF16)
        make_identity(nc, ident_bf16[:])
        norm_rows = const.tile([P, P], BF16)
        nc.vector.memset(norm_rows[:], 0.0)
        gelu_done = const.tile([P, 1], F32)
        nc.scalar.activation(out=gelu_done[:], in_=gelu_probe[:], func=ACT.Gelu_apprx_tanh)

        wo_raw = const.tile([P, PASSES, PACK, D], BF16)
        wo_rows = wo.rearrange("(s p t) c -> s p t c", s=PASSES, t=PACK)
        nc.sync.dma_start(out=wo_raw[:, 0], in_=wo_rows[0])
        load_attn(0)
        nc.sync.dma_start(out=wo_raw[:, 1], in_=wo_rows[1])
        nc.sync.dma_start(out=bias_rows[0:1, 0:D], in_=bo.rearrange("(o d) -> o d", o=1))
        nc.sync.dma_start(out=bias_rows[0:1, D : D + F], in_=b1.rearrange("(o f) -> o f", o=1))
        load_residual(0)
        load_attn(1)
        load_residual(1)
        for row, vector in ((0, ln2_gain), (PACK, ln2_bias)):
            nc.sync.dma_start(
                out=norm_rows[row : row + PACK, :].rearrange("t (b q) -> t b q", q=Q),
                in_=vector.rearrange("(b t q) -> t b q", t=PACK, q=Q),
            )
        w1_raw = const.tile([P, PACK, F], BF16)
        w1_rows = w1.rearrange("(b t q) f -> t b q f", t=PACK, q=Q)
        for t in range(PACK):
            nc.sync.dma_start(out=w1_raw[:, t, :], in_=w1_rows[t])
        for u in range(2, INPUT_BUFS):
            load_attn(u)
            load_residual(u)

        def regroup(copy, grouped, planes):
            copy(
                out=grouped.rearrange("p (c i t) -> p c t i", i=RUN, t=PACK),
                in_=planes.rearrange("p t (c i) -> p c t i", i=RUN),
            )

        wo_grouped = const.tile([P, PASSES, D * PACK], BF16, align_bytes=64)
        wo_codes = const.tile([P, PASSES, D], U32, align_bytes=64)
        wo_scales = const.tile([P, PASSES, D], U8, align_bytes=64)
        w1_grouped = const.tile([P, F * PACK], BF16, align_bytes=64)
        w1_codes = const.tile([P, F], U32, align_bytes=64)
        w1_scales = const.tile([P, F], U8, align_bytes=64)

        def prepare_wo():
            shared = 336
            regroup(nc.vector.tensor_copy, wo_grouped[:, 0, :], wo_raw[:, 0])
            regroup(nc.vector.tensor_copy, wo_grouped[:, 1, 0 : shared * PACK], wo_raw[:, 1, :, 0:shared])
            regroup(nc.scalar.copy, wo_grouped[:, 1, shared * PACK :], wo_raw[:, 1, :, shared:])
            for s in range(PASSES):
                nc.vector.quantize_mx(
                    out=wo_codes[:, s, :].bitcast(FP8X4), scales=wo_scales[:, s, :], in_=wo_grouped[:, s, :]
                )

        def regroup_w1():
            regroup(nc.scalar.copy, w1_grouped[:], w1_raw[:])

        def quantise_w1():
            nc.vector.quantize_mx(out=w1_codes[:].bitcast(FP8X4), scales=w1_scales[:], in_=w1_grouped[:])

        bo_all = const.tile([P, D], F32)
        b1_all = const.tile([P, F], F32)
        norm_cols = const.tile([P, 2 * PACK], F32)

        def spread_bias(spread, columns):
            bias_ps = psum.tile([P, D], F32, tag="acc")
            n = columns.stop - columns.start
            nc.tensor.matmul(out=bias_ps[:, 0:n], lhsT=ones[:], rhs=bias_rows[:, columns], start=True, stop=True)
            nc.scalar.copy(out=spread[:], in_=bias_ps[:, 0:n])

        def norm_columns():
            norm_ps = psum.tile([P, P], BF16, tag="planes")
            nc.tensor.transpose(norm_ps[:], norm_rows[:], ident_bf16[:])
            nc.scalar.copy(out=norm_cols[:], in_=norm_ps[:, 0 : 2 * PACK])

        def transpose_attn(u, i):
            at = psum.tile([P, PASSES * 2, P], F32, tag="at")
            for s in range(PASSES):
                start = i * (A // 2) + s * (K_PASS // 2)
                for w in range(2):
                    nc.tensor.transpose(
                        at[:, 2 * s + w, :],
                        live["attn_words", u][:, start + w : start + K_PASS // 2 : 2],
                        ident_f32[:],
                    )
            live["at", u, i] = at

        def group_attn(u):
            n = UNIT_TILES[u]
            a_grouped = work.tile([P, n * PASSES * P * PACK], BF16, align_bytes=64)
            words = a_grouped[:].bitcast(F32).rearrange("p (i s j u) -> p i s j u", i=n, s=PASSES, u=2)
            for i in range(n):
                nc.scalar.copy(
                    out=words[:, i], in_=live["at", u, i][:].rearrange("p (s u) j -> p s j u", u=2)
                )
            live["a_grouped", u] = a_grouped

        def quantise_attn(u):
            a_codes = work.tile([P, UNIT_TILES[u], PASSES, P], U32, align_bytes=64)
            a_scales = work.tile([P, UNIT_TILES[u], PASSES, P], U8, align_bytes=64)
            nc.vector.quantize_mx(
                out=a_codes[:].rearrange("p i s j -> p (i s j)").bitcast(FP8X4),
                scales=a_scales[:].rearrange("p i s j -> p (i s j)"),
                in_=live["a_grouped", u][:],
            )
            live["a_codes", u] = a_codes
            live["a_scales", u] = a_scales

        def project(u, i):
            acc = psum.tile([P, D], F32, tag="acc")
            for s in range(PASSES):
                nc.tensor.matmul_mx(
                    out=acc[:],
                    lhsT=live["a_codes", u][:, i, s, :].bitcast(FP8X4),
                    lhsT_scale=live["a_scales", u][:, i, s, :],
                    rhs=wo_codes[:, s, :].bitcast(FP8X4),
                    rhs_scale=wo_scales[:, s, :],
                    start=(s == 0),
                    stop=(s == PASSES - 1),
                )
            live["acc", u, i] = acc

        def release_gpsimd(u):
            res_bo = held.tile([P, UNIT_TILES[u], D], F32)
            live["res_bo", u] = res_bo
            if UNIT_TILES[u] == 2:
                nc.vector.memset(res_bo[:, 1, 0:1], 0.0)

        def add_bias_to_residual(u):
            nc.vector.tensor_tensor(
                out=live["res_bo", u][:, 0, :], in0=live["res", u][:, 0, :], in1=bo_all[:], op=ALU.add
            )

        def add_bias_on_gpsimd(u):
            if UNIT_TILES[u] == 2:
                nc.gpsimd.tensor_tensor(
                    out=live["res_bo", u][:, 1, :], in0=live["res", u][:, 1, :], in1=bo_all[:], op=ALU.add
                )

        def finish_x_mid(u):
            n = UNIT_TILES[u]
            x_mid = held.tile([P, n, D], F32)
            row_sum = held.tile([P, n], F32)
            for i in range(n):
                nc.vector.scalar_tensor_tensor(
                    out=x_mid[:, i, :],
                    in0=live["acc", u, i][:],
                    scalar=0.0,
                    in1=live["res_bo", u][:, i, :],
                    op0=ALU.add,
                    op1=ALU.add,
                    accum_out=row_sum[:, i : i + 1],
                )
            nc.sync.dma_start(out=unit_rows(out_0, u), in_=x_mid[:])
            live["x_mid", u] = x_mid
            live["row_sum", u] = row_sum

        def negate_mean(u):
            neg_mean = held.tile([P, UNIT_TILES[u]], F32)
            nc.scalar.mul(out=neg_mean[:], in_=live["row_sum", u][:], mul=-1.0 / D)
            live["neg_mean", u] = neg_mean

        def sum_squares(u):
            sq_sum = held.tile([P, UNIT_TILES[u]], F32)
            for i in range(UNIT_TILES[u]):
                squares = work.tile([P, D], BF16)
                nc.scalar.activation(
                    out=squares[:],
                    in_=live["x_mid", u][:, i, :],
                    func=ACT.Square,
                    bias=live["neg_mean", u][:, i : i + 1],
                    scale=1.0,
                    accum_out=sq_sum[:, i : i + 1],
                )
            live["sq_sum", u] = sq_sum

        def inverse_std(u):
            n = UNIT_TILES[u]
            var_eps = held.tile([P, n], F32)
            nc.scalar.activation(
                out=var_eps[:], in_=live["sq_sum", u][:], func=ACT.Identity, scale=1.0 / D, bias=eps_col[:]
            )
            rstd = held.tile([P, n], F32)
            nc.gpsimd.tensor_tensor(out=rstd[:], in0=var_eps[:], in1=minus_half[:, 0:n], op=ALU.pow)
            live["rstd", u] = rstd

        def by_plane(rows):
            return rows.rearrange("p (b t q) -> p t b q", t=PACK, q=Q)

        def planes_of(rows):
            return rows.rearrange("p (t b q) -> p t b q", t=PACK, q=Q)

        def scalar_normalises(u):
            return UNIT_TILES[u] == 2 and u % 2 > 0 and u < UNITS - 3

        def normalise_on_vector(u):
            normed = work.tile([P, UNIT_TILES[u], D], F32)
            for i in range(1 if scalar_normalises(u) else UNIT_TILES[u]):
                nc.vector.tensor_scalar(
                    out=planes_of(normed[:, i, :]),
                    in0=by_plane(live["x_mid", u][:, i, :]),
                    scalar1=live["neg_mean", u][:, i : i + 1],
                    scalar2=live["rstd", u][:, i : i + 1],
                    op0=ALU.add,
                    op1=ALU.mult,
                )
            live["normed", u] = normed

        def shift_of_tile_1(u):
            if not scalar_normalises(u):
                return
            shift = held.tile([P, 1], F32)
            nc.scalar.activation(
                out=shift[:], in_=live["neg_mean", u][:, 1:2], func=ACT.Identity, scale=live["rstd", u][:, 1:2]
            )
            live["shift", u] = shift

        def normalise_on_scalar(u):
            if not scalar_normalises(u):
                return
            nc.scalar.activation(
                out=planes_of(live["normed", u][:, 1, :]),
                in_=by_plane(live["x_mid", u][:, 1, :]),
                func=ACT.Identity,
                scale=live["rstd", u][:, 1:2],
                bias=live["shift", u][:],
            )

        def transpose_normed(u, half):
            planes = psum.tile([P, PACK // 2, UNIT_TILES[u], P], F32, tag="planes")
            for t2 in range(PACK // 2):
                t = half * (PACK // 2) + t2
                for i in range(UNIT_TILES[u]):
                    nc.tensor.transpose(
                        planes[:, t2, i, :], live["normed", u][:, i, t * P : (t + 1) * P], ident_f32[:]
                    )
            live["planes", u, half] = planes

        def gain_and_bias(u, half):
            if half == 0:
                h_planes = work.tile([P, PACK, UNIT_TILES[u] * P], BF16)
                live["h_planes", u] = h_planes
            for t in range(half * PACK // 2, (half + 1) * PACK // 2):
                nc.scalar.activation(
                    out=live["h_planes", u][:, t, :],
                    in_=live["planes", u, half][:, t % (PACK // 2)].rearrange("p i j -> p (i j)"),
                    func=ACT.Identity,
                    scale=norm_cols[:, t : t + 1],
                    bias=norm_cols[:, PACK + t : PACK + t + 1],
                )

        def group_h(u):
            h_grouped = work.tile([P, UNIT_TILES[u] * P * PACK], BF16, align_bytes=64)
            regroup(nc.vector.tensor_copy, h_grouped[:], live["h_planes", u][:])
            live["h_grouped", u] = h_grouped

        def quantise_h(u):
            h_codes = work.tile([P, UNIT_TILES[u] * P], U32, align_bytes=64)
            h_scales = work.tile([P, UNIT_TILES[u] * P], U8, align_bytes=64)
            nc.vector.quantize_mx(out=h_codes[:].bitcast(FP8X4), scales=h_scales[:], in_=live["h_grouped", u][:])
            live["h_codes", u] = h_codes
            live["h_scales", u] = h_scales

        def expand(u, i):
            if i == 0:
                acc2 = psum.tile([P, UNIT_TILES[u], F], F32, tag="acc2")
                live["acc2", u] = acc2
            nc.tensor.matmul_mx(
                out=live["acc2", u][:, i, :],
                lhsT=live["h_codes", u][:, i * P : (i + 1) * P].bitcast(FP8X4),
                lhsT_scale=live["h_scales", u][:, i * P : (i + 1) * P],
                rhs=w1_codes[:].bitcast(FP8X4),
                rhs_scale=w1_scales[:],
                start=True,
                stop=True,
            )

        def add_b1(u):
            n = UNIT_TILES[u]
            pre_gelu = work.tile([P, n, F], F32)
            nc.vector.tensor_tensor(
                out=pre_gelu[:],
                in0=live["acc2", u][:],
                in1=b1_all[:].unsqueeze(1).to_broadcast([P, n, F]),
                op=ALU.add,
            )
            live["pre_gelu", u] = pre_gelu

        def gelu_and_store(u):
            g_sb = held.tile([P, UNIT_TILES[u], F], F32)
            nc.scalar.activation(out=g_sb[:], in_=live["pre_gelu", u][:], func=ACT.Gelu_apprx_tanh)
            nc.sync.dma_start(out=unit_rows(out_1, u), in_=g_sb[:])

        def when_valid(stage, u, *part):
            if 0 <= u < UNITS:
                stage(u, *part)

        def for_tile(stage, u, i):
            if 0 <= u < UNITS and i < UNIT_TILES[u]:
                stage(u, i)

        with tc.manual_schedule():
            for slot in range(-2, UNITS + 7):
                if slot >= 0:
                    when_valid(load_attn, slot + INPUT_BUFS)
                    when_valid(load_residual, slot + INPUT_BUFS)
                if slot == -1:
                    prepare_wo()
                    spread_bias(bo_all, slice(0, D))
                if slot == 0:
                    spread_bias(b1_all, slice(D, D + F))
                    norm_columns()
                    regroup_w1()
                if slot == 1:
                    quantise_w1()
                for stage, u in ((project, slot), (expand, slot - 5)):
                    for_tile(stage, u, 0)
                    for_tile(stage, u, 1)
                for half in range(2):
                    when_valid(transpose_normed, slot - 3, half)
                for half in range(2):
                    for_tile(transpose_attn, slot + 2, half)
                when_valid(group_h, slot - 4)
                when_valid(release_gpsimd, slot + 1)
                when_valid(add_bias_to_residual, slot + 1)
                when_valid(add_bias_on_gpsimd, slot + 1)
                when_valid(finish_x_mid, slot)
                when_valid(quantise_attn, slot + 1)
                when_valid(quantise_h, slot - 4)
                when_valid(normalise_on_vector, slot - 2)
                when_valid(add_b1, slot - 5)
                when_valid(sum_squares, slot - 1)
                when_valid(gelu_and_store, slot - 6)
                when_valid(inverse_std, slot - 1)
                when_valid(shift_of_tile_1, slot - 2)
                when_valid(gain_and_bias, slot - 3, 0)
                when_valid(normalise_on_scalar, slot - 2)
                when_valid(gain_and_bias, slot - 3, 1)
                when_valid(negate_mean, slot)
                when_valid(group_attn, slot + 2)
